import numpy as np
import ml_dtypes

BF16 = ml_dtypes.bfloat16


def bf(x):
    return np.asarray(x, np.float32).astype(BF16)


def f32(x):
    return np.asarray(x, np.float32)


def f64(x):
    return np.asarray(x).astype(np.float64)


def striped(idx):
    return np.tile(idx.reshape(-1, 16).T, (8, 1))


D, S, N, L, B, V, K = 256, 4096, 2048, 8, 256, 4096, 64
PE_BASE = 10000.0
TAB_SCALE = 0.2


def pos_table():
    pos = np.arange(L, dtype=np.float64)[None, :]
    div = np.exp(np.arange(0, D, 2, dtype=np.float64) * (-np.log(PE_BASE) / D))[:, None]
    pe = np.zeros((D, L))
    pe[0::2] = np.sin(div * pos)
    pe[1::2] = np.cos(div * pos)
    return np.repeat(pe, B, axis=1)


def setup_inputs():
    base = f32(np.random.standard_normal((D, S)))
    rows = np.stack([np.random.permutation(V)[:K] for _ in range(L * B)]).reshape(L, B, K).transpose(0, 2, 1)
    mat = np.zeros((L, V, B))
    np.put_along_axis(mat, rows, np.random.random((L, K, B)), axis=1)
    val_tab = bf(TAB_SCALE * np.random.standard_normal((V, D)))
    return {"base": base, "val_mat": bf(mat), "val_tab": val_tab, "pos_enc": f32(pos_table()), "offs": striped(np.random.permutation(S)[:N])}


def reference(base, val_mat, val_tab, pos_enc, offs):
    idx = offs[:16].T.reshape(-1)
    mat = f64(val_mat)
    tab = f64(val_tab)
    emb = np.concatenate([tab.T @ mat[t] for t in range(L)], axis=1)
    out = f64(base).copy()
    out[:, idx] = emb + f64(pos_enc)
    return out

@@ -1,0 +1,68 @@
+import concourse.mybir as mybir
+
+BF16, F32, U16 = mybir.dt.bfloat16, mybir.dt.float32, mybir.dt.uint16
+ADD = mybir.AluOpType.add
+COPY = mybir.ActivationFunctionType.Copy
+
+P = 128
+D = 256
+S = 4096
+L = 8
+B = 256
+V = 4096
+N = L * B
+KT = V // P
+KQ = 8
+PAIR = 2
+
+FLOPS = 2 * L * V * D * B
+
+
+def tile_progwalktokembedwithval_b_kernel(tc, base, val_mat, val_tab, pos_enc, offs, out):
+    nc = tc.nc
+    mat_view = val_mat.rearrange("t (p k) u -> p t k u", k=KT)
+    tab_view = val_tab.rearrange("(p k) c -> p k c", k=KT)
+
+    with (
+        tc.tile_pool(name="held", bufs=1) as held,
+        tc.psum_pool(name="psum", bufs=4) as psum,
+    ):
+        offsets = held.tile([P, N // 16], U16, name="offsets")
+        nc.sync.dma_start(offsets[:], offs)
+
+        tab = []
+        for q in range(KT // KQ):
+            tab_q = held.tile([P, KQ, D], BF16, name=f"tab{q}")
+            nc.scalar.dma_start(tab_q[:], tab_view[:, q * KQ : (q + 1) * KQ, :])
+            tab.append(tab_q)
+        mat = []
+        for j in range(L // PAIR):
+            mat.append([])
+            for q in range(KT // KQ):
+                mat_jq = held.tile([P, PAIR, KQ, B], BF16, name=f"mat{j}_{q}")
+                nc.sync.dma_start(mat_jq[:], mat_view[:, j * PAIR : (j + 1) * PAIR, q * KQ : (q + 1) * KQ, :])
+                mat[j].append(mat_jq)
+        window, pos = [], []
+        for c in range(D // P):
+            window_c = held.tile([P, S], F32, name=f"window{c}")
+            nc.sync.dma_start(window_c[:], base[c * P : (c + 1) * P, :])
+            window.append(window_c)
+            pos_c = held.tile([P, N], F32, name=f"pos{c}")
+            nc.sync.dma_start(pos_c[:], pos_enc[c * P : (c + 1) * P, :])
+            pos.append(pos_c)
+
+        for c in range(D // P):
+            emb = held.tile([P, N], F32, name=f"emb{c}")
+            for j in range(L // PAIR):
+                acc = psum.tile([P, PAIR * B], F32, name="acc")
+                for k in range(KT):
+                    nc.tensor.matmul(
+                        acc[:].rearrange("p (t u) -> p t u", t=PAIR),
+                        tab[k // KQ][:, k % KQ, c * P : (c + 1) * P],
+                        mat[j][k // KQ][:, :, k % KQ, :],
+                        start=(k == 0),
+                        stop=(k == KT - 1),
+                    )
+                nc.scalar.activation(emb[:, j * PAIR * B : (j + 1) * PAIR * B], acc[:], COPY)
+            nc.vector.tensor_tensor(window[c][:].indirect(offsets[:]), emb[:], pos[c][:], ADD)
+            nc.sync.dma_start(out[c * P : (c + 1) * P, :], window[c][:])

@@ -51,18 +51,25 @@ def tile_progwalktokembedwithval_b_kernel(tc, base, val_mat, val_tab, pos_enc, o
             nc.sync.dma_start(pos_c[:], pos_enc[c * P : (c + 1) * P, :])
             pos.append(pos_c)
 
-        for c in range(D // P):
-            emb = held.tile([P, N], F32, name=f"emb{c}")
-            for j in range(L // PAIR):
-                acc = psum.tile([P, PAIR * B], F32, name="acc")
-                for k in range(KT):
+        emb = [held.tile([P, N], F32, name=f"emb{c}") for c in range(D // P)]
+
+        def multiply(j, blocks):
+            acc = {c: psum.tile([P, PAIR * B], F32, name="acc") for c in blocks}
+            for k in range(KT):
+                for c in blocks:
                     nc.tensor.matmul(
-                        acc[:].rearrange("p (t u) -> p t u", t=PAIR),
+                        acc[c][:].rearrange("p (t u) -> p t u", t=PAIR),
                         tab[k // KQ][:, k % KQ, c * P : (c + 1) * P],
                         mat[j][k // KQ][:, :, k % KQ, :],
                         start=(k == 0),
                         stop=(k == KT - 1),
                     )
-                nc.scalar.activation(emb[:, j * PAIR * B : (j + 1) * PAIR * B], acc[:], COPY)
-            nc.vector.tensor_tensor(window[c][:].indirect(offsets[:]), emb[:], pos[c][:], ADD)
+            for c in blocks:
+                nc.scalar.activation(emb[c][:, j * PAIR * B : (j + 1) * PAIR * B], acc[c][:], COPY)
+
+        multiply(0, (0, 1))
+        for c in range(D // P):
+            for j in range(1, L // PAIR):
+                multiply(j, (c,))
+            nc.vector.tensor_tensor(window[c][:].indirect(offsets[:]), emb[c][:], pos[c][:], ADD)
             nc.sync.dma_start(out[c * P : (c + 1) * P, :], window[c][:])

@@ -12,10 +12,17 @@ B = 256
 V = 4096
 N = L * B
 KT = V // P
-KQ = 8
 PAIR = 2
+PAIRS = L // PAIR
+EARLY = 4
+LATER = 8
+BLOCKS = D // P
 
 FLOPS = 2 * L * V * D * B
+
+
+def pieces(step):
+    return [(k0, k0 + step) for k0 in range(0, KT, step)]
 
 
 def tile_progwalktokembedwithval_b_kernel(tc, base, val_mat, val_tab, pos_enc, offs, out):
@@ -27,31 +34,22 @@ def tile_progwalktokembedwithval_b_kernel(tc, base, val_mat, val_tab, pos_enc, o
         tc.tile_pool(name="held", bufs=1) as held,
         tc.psum_pool(name="psum", bufs=4) as psum,
     ):
+        tab = held.tile([P, KT, D], BF16, name="tab")
+        for k0, k1 in pieces(EARLY):
+            nc.scalar.dma_start(tab[:, k0:k1, :], tab_view[:, k0:k1, :])
+        mat = [held.tile([P, PAIR, KT, B], BF16, name=f"mat{j}") for j in range(PAIRS)]
+        for j in range(PAIRS):
+            for k0, k1 in pieces(EARLY if j == 0 else LATER):
+                nc.sync.dma_start(mat[j][:, :, k0:k1, :], mat_view[:, j * PAIR : (j + 1) * PAIR, k0:k1, :])
         offsets = held.tile([P, N // 16], U16, name="offsets")
         nc.sync.dma_start(offsets[:], offs)
+        window = [held.tile([P, S], F32, name=f"window{c}") for c in range(BLOCKS)]
+        pos = [held.tile([P, N], F32, name=f"pos{c}") for c in range(BLOCKS)]
+        for c in range(BLOCKS):
+            nc.sync.dma_start(window[c][:], base[c * P : (c + 1) * P, :])
+            nc.sync.dma_start(pos[c][:], pos_enc[c * P : (c + 1) * P, :])
 
-        tab = []
-        for q in range(KT // KQ):
-            tab_q = held.tile([P, KQ, D], BF16, name=f"tab{q}")
-            nc.scalar.dma_start(tab_q[:], tab_view[:, q * KQ : (q + 1) * KQ, :])
-            tab.append(tab_q)
-        mat = []
-        for j in range(L // PAIR):
-            mat.append([])
-            for q in range(KT // KQ):
-                mat_jq = held.tile([P, PAIR, KQ, B], BF16, name=f"mat{j}_{q}")
-                nc.sync.dma_start(mat_jq[:], mat_view[:, j * PAIR : (j + 1) * PAIR, q * KQ : (q + 1) * KQ, :])
-                mat[j].append(mat_jq)
-        window, pos = [], []
-        for c in range(D // P):
-            window_c = held.tile([P, S], F32, name=f"window{c}")
-            nc.sync.dma_start(window_c[:], base[c * P : (c + 1) * P, :])
-            window.append(window_c)
-            pos_c = held.tile([P, N], F32, name=f"pos{c}")
-            nc.sync.dma_start(pos_c[:], pos_enc[c * P : (c + 1) * P, :])
-            pos.append(pos_c)
-
-        emb = [held.tile([P, N], F32, name=f"emb{c}") for c in range(D // P)]
+        emb = [held.tile([P, N], F32, name=f"emb{c}") for c in range(BLOCKS)]
 
         def multiply(j, blocks):
             acc = {c: psum.tile([P, PAIR * B], F32, name="acc") for c in blocks}
@@ -59,17 +57,18 @@ def tile_progwalktokembedwithval_b_kernel(tc, base, val_mat, val_tab, pos_enc, o
                 for c in blocks:
                     nc.tensor.matmul(
                         acc[c][:].rearrange("p (t u) -> p t u", t=PAIR),
-                        tab[k // KQ][:, k % KQ, c * P : (c + 1) * P],
-                        mat[j][k // KQ][:, :, k % KQ, :],
+                        tab[:, k, c * P : (c + 1) * P],
+                        mat[j][:, :, k, :],
                         start=(k == 0),
                         stop=(k == KT - 1),
                     )
             for c in blocks:
                 nc.scalar.activation(emb[c][:, j * PAIR * B : (j + 1) * PAIR * B], acc[c][:], COPY)
 
-        multiply(0, (0, 1))
-        for c in range(D // P):
-            for j in range(1, L // PAIR):
+        for j in range(PAIRS // 2):
+            multiply(j, range(BLOCKS))
+        for c in range(BLOCKS):
+            for j in range(PAIRS // 2, PAIRS):
                 multiply(j, (c,))
             nc.vector.tensor_tensor(window[c][:].indirect(offsets[:]), emb[c][:], pos[c][:], ADD)
             nc.sync.dma_start(out[c * P : (c + 1) * P, :], window[c][:])

@@ -17,6 +17,8 @@ PAIRS = L // PAIR
 EARLY = 4
 LATER = 8
 BLOCKS = D // P
+BANK = 512
+WARM = 6
 
 FLOPS = 2 * L * V * D * B
 
@@ -48,6 +50,12 @@ def tile_progwalktokembedwithval_b_kernel(tc, base, val_mat, val_tab, pos_enc, o
         for c in range(BLOCKS):
             nc.sync.dma_start(window[c][:], base[c * P : (c + 1) * P, :])
             nc.sync.dma_start(pos[c][:], pos_enc[c * P : (c + 1) * P, :])
+
+        zeros = held.tile([P, BANK], BF16, name="zeros")
+        nc.vector.memset(zeros[:], 0.0)
+        unread = psum.tile([P, BANK], F32, name="unread", bufs=1)
+        for i in range(WARM):
+            nc.tensor.matmul(unread[:], zeros[:, :P], zeros[:], start=True, stop=True)
 
         emb = [held.tile([P, N], F32, name=f"emb{c}") for c in range(BLOCKS)]
 

@@ -14,11 +14,9 @@ N = L * B
 KT = V // P
 PAIR = 2
 PAIRS = L // PAIR
-EARLY = 4
+EARLY = 2
 LATER = 8
 BLOCKS = D // P
-BANK = 512
-WARM = 6
 
 FLOPS = 2 * L * V * D * B
 
@@ -34,15 +32,21 @@ def tile_progwalktokembedwithval_b_kernel(tc, base, val_mat, val_tab, pos_enc, o
 
     with (
         tc.tile_pool(name="held", bufs=1) as held,
-        tc.psum_pool(name="psum", bufs=4) as psum,
+        tc.psum_pool(name="psum", bufs=PAIRS * BLOCKS) as psum,
     ):
         tab = held.tile([P, KT, D], BF16, name="tab")
+        mat = [held.tile([P, PAIR, KT, B], BF16, name=f"mat{j}") for j in range(PAIRS)]
+
+        def load_mat(j, k0, k1):
+            nc.sync.dma_start(mat[j][:, :, k0:k1, :], mat_view[:, j * PAIR : (j + 1) * PAIR, k0:k1, :])
+
         for k0, k1 in pieces(EARLY):
             nc.scalar.dma_start(tab[:, k0:k1, :], tab_view[:, k0:k1, :])
-        mat = [held.tile([P, PAIR, KT, B], BF16, name=f"mat{j}") for j in range(PAIRS)]
-        for j in range(PAIRS):
-            for k0, k1 in pieces(EARLY if j == 0 else LATER):
-                nc.sync.dma_start(mat[j][:, :, k0:k1, :], mat_view[:, j * PAIR : (j + 1) * PAIR, k0:k1, :])
+            for j in range(PAIRS // 2):
+                load_mat(j, k0, k1)
+        for j in range(PAIRS // 2, PAIRS):
+            for k0, k1 in pieces(LATER):
+                load_mat(j, k0, k1)
         offsets = held.tile([P, N // 16], U16, name="offsets")
         nc.sync.dma_start(offsets[:], offs)
         window = [held.tile([P, S], F32, name=f"window{c}") for c in range(BLOCKS)]
@@ -51,32 +55,25 @@ def tile_progwalktokembedwithval_b_kernel(tc, base, val_mat, val_tab, pos_enc, o
             nc.sync.dma_start(window[c][:], base[c * P : (c + 1) * P, :])
             nc.sync.dma_start(pos[c][:], pos_enc[c * P : (c + 1) * P, :])
 
-        zeros = held.tile([P, BANK], BF16, name="zeros")
-        nc.vector.memset(zeros[:], 0.0)
-        unread = psum.tile([P, BANK], F32, name="unread", bufs=1)
-        for i in range(WARM):
-            nc.tensor.matmul(unread[:], zeros[:, :P], zeros[:], start=True, stop=True)
-
         emb = [held.tile([P, N], F32, name=f"emb{c}") for c in range(BLOCKS)]
 
-        def multiply(j, blocks):
-            acc = {c: psum.tile([P, PAIR * B], F32, name="acc") for c in blocks}
+        def multiply(pairs, blocks):
+            acc = {(j, c): psum.tile([P, PAIR * B], F32, name="acc") for j in pairs for c in blocks}
             for k in range(KT):
-                for c in blocks:
+                for j, c in acc:
                     nc.tensor.matmul(
-                        acc[c][:].rearrange("p (t u) -> p t u", t=PAIR),
+                        acc[j, c][:].rearrange("p (t u) -> p t u", t=PAIR),
                         tab[:, k, c * P : (c + 1) * P],
                         mat[j][:, :, k, :],
                         start=(k == 0),
                         stop=(k == KT - 1),
                     )
-            for c in blocks:
-                nc.scalar.activation(emb[c][:, j * PAIR * B : (j + 1) * PAIR * B], acc[c][:], COPY)
+            for j, c in acc:
+                nc.scalar.activation(emb[c][:, j * PAIR * B : (j + 1) * PAIR * B], acc[j, c][:], COPY)
 
-        for j in range(PAIRS // 2):
-            multiply(j, range(BLOCKS))
+        multiply(range(PAIRS // 2), range(BLOCKS))
         for c in range(BLOCKS):
             for j in range(PAIRS // 2, PAIRS):
-                multiply(j, (c,))
+                multiply((j,), (c,))
             nc.vector.tensor_tensor(window[c][:].indirect(offsets[:]), emb[c][:], pos[c][:], ADD)
             nc.sync.dma_start(out[c * P : (c + 1) * P, :], window[c][:])

@@ -21,8 +21,8 @@ BLOCKS = D // P
 FLOPS = 2 * L * V * D * B
 
 
-def pieces(step):
-    return [(k0, k0 + step) for k0 in range(0, KT, step)]
+def pieces(step, start=0):
+    return [(k0, k0 + step) for k0 in range(start, KT, step)]
 
 
 def tile_progwalktokembedwithval_b_kernel(tc, base, val_mat, val_tab, pos_enc, offs, out):
@@ -40,7 +40,7 @@ def tile_progwalktokembedwithval_b_kernel(tc, base, val_mat, val_tab, pos_enc, o
         def load_mat(j, k0, k1):
             nc.sync.dma_start(mat[j][:, :, k0:k1, :], mat_view[:, j * PAIR : (j + 1) * PAIR, k0:k1, :])
 
-        for k0, k1 in pieces(EARLY):
+        for k0, k1 in [(0, 1), (1, 2)] + pieces(EARLY, start=2):
             nc.scalar.dma_start(tab[:, k0:k1, :], tab_view[:, k0:k1, :])
             for j in range(PAIRS // 2):
                 load_mat(j, k0, k1)
@@ -57,23 +57,25 @@ def tile_progwalktokembedwithval_b_kernel(tc, base, val_mat, val_tab, pos_enc, o
 
         emb = [held.tile([P, N], F32, name=f"emb{c}") for c in range(BLOCKS)]
 
-        def multiply(pairs, blocks):
-            acc = {(j, c): psum.tile([P, PAIR * B], F32, name="acc") for j in pairs for c in blocks}
+        def multiply(spans, blocks):
+            acc = {(t0, nt, c): psum.tile([P, nt * B], F32, name="acc") for t0, nt in spans for c in blocks}
             for k in range(KT):
-                for j, c in acc:
+                for (t0, nt, c), bank in acc.items():
+                    j, t = divmod(t0, PAIR)
                     nc.tensor.matmul(
-                        acc[j, c][:].rearrange("p (t u) -> p t u", t=PAIR),
+                        bank[:].rearrange("p (t u) -> p t u", t=nt),
                         tab[:, k, c * P : (c + 1) * P],
-                        mat[j][:, :, k, :],
+                        mat[j][:, t : t + nt, k, :],
                         start=(k == 0),
                         stop=(k == KT - 1),
                     )
-            for j, c in acc:
-                nc.scalar.activation(emb[c][:, j * PAIR * B : (j + 1) * PAIR * B], acc[j, c][:], COPY)
+            for (t0, nt, c), bank in acc.items():
+                nc.scalar.activation(emb[c][:, t0 * B : (t0 + nt) * B], bank[:], COPY)
 
-        multiply(range(PAIRS // 2), range(BLOCKS))
+        multiply([(0, PAIR), (PAIR, PAIR)], range(BLOCKS))
         for c in range(BLOCKS):
-            for j in range(PAIRS // 2, PAIRS):
-                multiply((j,), (c,))
+            multiply([(L - 2 * PAIR, PAIR)], (c,))
+            for t in range(L - PAIR, L):
+                multiply([(t, 1)], (c,))
             nc.vector.tensor_tensor(window[c][:].indirect(offsets[:]), emb[c][:], pos[c][:], ADD)
             nc.sync.dma_start(out[c * P : (c + 1) * P, :], window[c][:])

@@ -21,8 +21,15 @@ BLOCKS = D // P
 FLOPS = 2 * L * V * D * B
 
 
-def pieces(step, start=0):
-    return [(k0, k0 + step) for k0 in range(start, KT, step)]
+def pieces(step, start=0, end=KT):
+    return [(k0, k0 + step) for k0 in range(start, end, step)]
+
+
+def halving(start):
+    cuts = [start]
+    while KT - cuts[-1] > 1:
+        cuts.append(cuts[-1] + (KT - cuts[-1]) // 2)
+    return list(zip(cuts, cuts[1:] + [KT]))
 
 
 def tile_progwalktokembedwithval_b_kernel(tc, base, val_mat, val_tab, pos_enc, offs, out):
@@ -40,13 +47,14 @@ def tile_progwalktokembedwithval_b_kernel(tc, base, val_mat, val_tab, pos_enc, o
         def load_mat(j, k0, k1):
             nc.sync.dma_start(mat[j][:, :, k0:k1, :], mat_view[:, j * PAIR : (j + 1) * PAIR, k0:k1, :])
 
-        for k0, k1 in [(0, 1), (1, 2)] + pieces(EARLY, start=2):
+        for k0, k1 in [(0, 1), (1, 2)] + pieces(EARLY, start=2, end=KT - EARLY) + halving(KT - EARLY):
             nc.scalar.dma_start(tab[:, k0:k1, :], tab_view[:, k0:k1, :])
             for j in range(PAIRS // 2):
                 load_mat(j, k0, k1)
-        for j in range(PAIRS // 2, PAIRS):
-            for k0, k1 in pieces(LATER):
-                load_mat(j, k0, k1)
+        for k0, k1 in pieces(LATER):
+            load_mat(PAIRS - 2, k0, k1)
+        for k0, k1 in pieces(LATER, end=KT - LATER) + halving(KT - LATER):
+            load_mat(PAIRS - 1, k0, k1)
         offsets = held.tile([P, N // 16], U16, name="offsets")
         nc.sync.dma_start(offsets[:], offs)
         window = [held.tile([P, S], F32, name=f"window{c}") for c in range(BLOCKS)]

@@ -83,7 +83,10 @@ def tile_progwalktokembedwithval_b_kernel(tc, base, val_mat, val_tab, pos_enc, o
         multiply([(0, PAIR), (PAIR, PAIR)], range(BLOCKS))
         for c in range(BLOCKS):
             multiply([(L - 2 * PAIR, PAIR)], (c,))
-            for t in range(L - PAIR, L):
-                multiply([(t, 1)], (c,))
+            if c < BLOCKS - 1:
+                multiply([(L - PAIR, PAIR)], (c,))
+            else:
+                for t in range(L - PAIR, L):
+                    multiply([(t, 1)], (c,))
             nc.vector.tensor_tensor(window[c][:].indirect(offsets[:]), emb[c][:], pos[c][:], ADD)
             nc.sync.dma_start(out[c * P : (c + 1) * P, :], window[c][:])

@@ -17,6 +17,7 @@ PAIRS = L // PAIR
 EARLY = 2
 LATER = 8
 BLOCKS = D // P
+LAST = 32
 
 FLOPS = 2 * L * V * D * B
 
@@ -63,30 +64,29 @@ def tile_progwalktokembedwithval_b_kernel(tc, base, val_mat, val_tab, pos_enc, o
             nc.sync.dma_start(window[c][:], base[c * P : (c + 1) * P, :])
             nc.sync.dma_start(pos[c][:], pos_enc[c * P : (c + 1) * P, :])
 
-        emb = [held.tile([P, N], F32, name=f"emb{c}") for c in range(BLOCKS)]
+        emb = [held.tile([P, L, B], F32, name=f"emb{c}") for c in range(BLOCKS)]
 
-        def multiply(spans, blocks):
-            acc = {(t0, nt, c): psum.tile([P, nt * B], F32, name="acc") for t0, nt in spans for c in blocks}
+        def multiply(pairs, blocks, u0=0, u1=B):
+            acc = {(j, c): psum.tile([P, PAIR, u1 - u0], F32, name="acc") for j in pairs for c in blocks}
             for k in range(KT):
-                for (t0, nt, c), bank in acc.items():
-                    j, t = divmod(t0, PAIR)
+                for (j, c), bank in acc.items():
                     nc.tensor.matmul(
-                        bank[:].rearrange("p (t u) -> p t u", t=nt),
+                        bank[:],
                         tab[:, k, c * P : (c + 1) * P],
-                        mat[j][:, t : t + nt, k, :],
+                        mat[j][:, :, k, u0:u1],
                         start=(k == 0),
                         stop=(k == KT - 1),
                     )
-            for (t0, nt, c), bank in acc.items():
-                nc.scalar.activation(emb[c][:, t0 * B : (t0 + nt) * B], bank[:], COPY)
+            for (j, c), bank in acc.items():
+                nc.scalar.activation(emb[c][:, j * PAIR : (j + 1) * PAIR, u0:u1], bank[:], COPY)
 
-        multiply([(0, PAIR), (PAIR, PAIR)], range(BLOCKS))
+        multiply(range(PAIRS // 2), range(BLOCKS))
         for c in range(BLOCKS):
-            multiply([(L - 2 * PAIR, PAIR)], (c,))
+            multiply((PAIRS - 2,), (c,))
             if c < BLOCKS - 1:
-                multiply([(L - PAIR, PAIR)], (c,))
+                multiply((PAIRS - 1,), (c,))
             else:
-                for t in range(L - PAIR, L):
-                    multiply([(t, 1)], (c,))
-            nc.vector.tensor_tensor(window[c][:].indirect(offsets[:]), emb[c][:], pos[c][:], ADD)
+                multiply((PAIRS - 1,), (c,), 0, B - LAST)
+                multiply((PAIRS - 1,), (c,), B - LAST, B)
+            nc.vector.tensor_tensor(window[c][:].indirect(offsets[:]), emb[c][:].rearrange("p t u -> p (t u)"), pos[c][:], ADD)
             nc.sync.dma_start(out[c * P : (c + 1) * P, :], window[c][:])

@@ -48,7 +48,8 @@ def tile_progwalktokembedwithval_b_kernel(tc, base, val_mat, val_tab, pos_enc, o
         def load_mat(j, k0, k1):
             nc.sync.dma_start(mat[j][:, :, k0:k1, :], mat_view[:, j * PAIR : (j + 1) * PAIR, k0:k1, :])
 
-        for k0, k1 in [(0, 1), (1, 2)] + pieces(EARLY, start=2, end=KT - EARLY) + halving(KT - EARLY):
+        chunks = [(0, 1), (1, 2)] + pieces(EARLY, start=2, end=KT - EARLY) + halving(KT - EARLY)
+        for k0, k1 in chunks:
             nc.scalar.dma_start(tab[:, k0:k1, :], tab_view[:, k0:k1, :])
             for j in range(PAIRS // 2):
                 load_mat(j, k0, k1)
@@ -66,21 +67,23 @@ def tile_progwalktokembedwithval_b_kernel(tc, base, val_mat, val_tab, pos_enc, o
 
         emb = [held.tile([P, L, B], F32, name=f"emb{c}") for c in range(BLOCKS)]
 
-        def multiply(pairs, blocks, u0=0, u1=B):
+        def multiply(pairs, blocks, u0=0, u1=B, chunks=((0, KT),)):
             acc = {(j, c): psum.tile([P, PAIR, u1 - u0], F32, name="acc") for j in pairs for c in blocks}
-            for k in range(KT):
-                for (j, c), bank in acc.items():
-                    nc.tensor.matmul(
-                        bank[:],
-                        tab[:, k, c * P : (c + 1) * P],
-                        mat[j][:, :, k, u0:u1],
-                        start=(k == 0),
-                        stop=(k == KT - 1),
-                    )
+            for k0, k1 in chunks:
+                for j in pairs:
+                    for k in range(k0, k1):
+                        for c in blocks:
+                            nc.tensor.matmul(
+                                acc[j, c][:],
+                                tab[:, k, c * P : (c + 1) * P],
+                                mat[j][:, :, k, u0:u1],
+                                start=(k == 0),
+                                stop=(k == KT - 1),
+                            )
             for (j, c), bank in acc.items():
                 nc.scalar.activation(emb[c][:, j * PAIR : (j + 1) * PAIR, u0:u1], bank[:], COPY)
 
-        multiply(range(PAIRS // 2), range(BLOCKS))
+        multiply(range(PAIRS // 2), range(BLOCKS), chunks=chunks)
         for c in range(BLOCKS):
             multiply((PAIRS - 2,), (c,))
             if c < BLOCKS - 1:

import concourse.mybir as mybir

BF16, F32, U16 = mybir.dt.bfloat16, mybir.dt.float32, mybir.dt.uint16
ADD = mybir.AluOpType.add
COPY = mybir.ActivationFunctionType.Copy

P = 128
D = 256
S = 4096
L = 8
B = 256
V = 4096
N = L * B
KT = V // P
PAIR = 2
PAIRS = L // PAIR
EARLY = 2
LATER = 8
BLOCKS = D // P
LAST = 32

FLOPS = 2 * L * V * D * B


def pieces(step, start=0, end=KT):
    return [(k0, k0 + step) for k0 in range(start, end, step)]


def halving(start):
    cuts = [start]
    while KT - cuts[-1] > 1:
        cuts.append(cuts[-1] + (KT - cuts[-1]) // 2)
    return list(zip(cuts, cuts[1:] + [KT]))


def tile_progwalktokembedwithval_b_kernel(tc, base, val_mat, val_tab, pos_enc, offs, out):
    nc = tc.nc
    mat_view = val_mat.rearrange("t (p k) u -> p t k u", k=KT)
    tab_view = val_tab.rearrange("(p k) c -> p k c", k=KT)

    with (
        tc.tile_pool(name="held", bufs=1) as held,
        tc.psum_pool(name="psum", bufs=PAIRS * BLOCKS) as psum,
    ):
        tab = held.tile([P, KT, D], BF16, name="tab")
        mat = [held.tile([P, PAIR, KT, B], BF16, name=f"mat{j}") for j in range(PAIRS)]

        def load_mat(j, k0, k1):
            nc.sync.dma_start(mat[j][:, :, k0:k1, :], mat_view[:, j * PAIR : (j + 1) * PAIR, k0:k1, :])

        chunks = [(0, 1), (1, 2)] + pieces(EARLY, start=2, end=KT - EARLY) + halving(KT - EARLY)
        for k0, k1 in chunks:
            nc.scalar.dma_start(tab[:, k0:k1, :], tab_view[:, k0:k1, :])
            for j in range(PAIRS // 2):
                load_mat(j, k0, k1)
        for k0, k1 in pieces(LATER):
            load_mat(PAIRS - 2, k0, k1)
        for k0, k1 in pieces(LATER, end=KT - LATER) + halving(KT - LATER):
            load_mat(PAIRS - 1, k0, k1)
        offsets = held.tile([P, N // 16], U16, name="offsets")
        nc.sync.dma_start(offsets[:], offs)
        window = [held.tile([P, S], F32, name=f"window{c}") for c in range(BLOCKS)]
        pos = [held.tile([P, N], F32, name=f"pos{c}") for c in range(BLOCKS)]
        for c in range(BLOCKS):
            nc.sync.dma_start(window[c][:], base[c * P : (c + 1) * P, :])
            nc.sync.dma_start(pos[c][:], pos_enc[c * P : (c + 1) * P, :])

        emb = [held.tile([P, L, B], F32, name=f"emb{c}") for c in range(BLOCKS)]

        def multiply(pairs, blocks, u0=0, u1=B, chunks=((0, KT),)):
            acc = {(j, c): psum.tile([P, PAIR, u1 - u0], F32, name="acc") for j in pairs for c in blocks}
            for k0, k1 in chunks:
                for j in pairs:
                    for k in range(k0, k1):
                        for c in blocks:
                            nc.tensor.matmul(
                                acc[j, c][:],
                                tab[:, k, c * P : (c + 1) * P],
                                mat[j][:, :, k, u0:u1],
                                start=(k == 0),
                                stop=(k == KT - 1),
                            )
            for (j, c), bank in acc.items():
                nc.scalar.activation(emb[c][:, j * PAIR : (j + 1) * PAIR, u0:u1], bank[:], COPY)

        multiply(range(PAIRS // 2), range(BLOCKS), chunks=chunks)
        for c in range(BLOCKS):
            multiply((PAIRS - 2,), (c,))
            if c < BLOCKS - 1:
                multiply((PAIRS - 1,), (c,))
            else:
                multiply((PAIRS - 1,), (c,), 0, B - LAST)
                multiply((PAIRS - 1,), (c,), B - LAST, B)
            nc.vector.tensor_tensor(window[c][:].indirect(offsets[:]), emb[c][:].rearrange("p t u -> p (t u)"), pos[c][:], ADD)
            nc.sync.dma_start(out[c * P : (c + 1) * P, :], window[c][:])
